import numpy as np
import ml_dtypes


def mxq(x, axis, fmt="e4m3"):
    dtype, down = {"e4m3": (ml_dtypes.float8_e4m3fn, 7), "e5m2": (ml_dtypes.float8_e5m2, 14)}[fmt]
    v = np.moveaxis(np.asarray(x, np.float32).astype(ml_dtypes.bfloat16).astype(np.float64), axis, -1)
    blocks = v.reshape(v.shape[:-1] + (-1, 32))
    amax = np.abs(blocks).max(-1, keepdims=True)
    byte = np.maximum(np.where(amax > 0, np.frexp(amax)[1] - 1 + 127, 0) - down, 1)
    scale = np.exp2(byte - 127.0)
    codes = (blocks / scale).astype(np.float32).astype(dtype).astype(np.float64)
    return np.moveaxis((codes * scale).reshape(v.shape), -1, axis)


WIDE = False


def mx_kscale(k):
    if not WIDE:
        return np.ones(k)
    levels = np.array([20, -20, 10, -10, 0])
    a = np.random.permutation(np.resize(levels, k // 512 * 4)).reshape(k // 512, 4)
    idx = np.arange(k)
    return np.exp2(a[idx // 512, idx % 128 // 32])


BF16 = ml_dtypes.bfloat16


def bf(x):
    return np.asarray(x, np.float32).astype(BF16)


def f64(x):
    return np.asarray(x).astype(np.float64)


B, HEAD, NUM_EXPERTS, HEAD_DIM = 1024, 2, 3, 512
EPS = 1e-5
VAR0 = 3e-4


def sigmoid(v):
    return 1.0 / (1.0 + np.exp(-v))


def pre_activation(x1, x2, x3, W, b):
    n = x1.shape[0]
    xs = np.stack([f64(x1).reshape(n, HEAD, HEAD_DIM),
                   f64(x2).reshape(n, HEAD, HEAD_DIM),
                   f64(x3).reshape(n, HEAD, HEAD_DIM)], axis=2)
    y = xs.transpose(1, 2, 0, 3) @ f64(W).transpose(0, 1, 3, 2)
    y = y.transpose(2, 1, 0, 3) + f64(b).transpose(1, 0, 2)
    return y.reshape(n, NUM_EXPERTS * HEAD * HEAD_DIM)


def setup_inputs():
    s = mx_kscale(B)[:, None]
    p = (HEAD, NUM_EXPERTS, HEAD_DIM)
    x10 = bf(np.random.standard_normal((B, HEAD * HEAD_DIM)))
    x20 = bf(np.random.standard_normal((B, HEAD * HEAD_DIM)))
    x30 = bf(np.random.standard_normal((B, HEAD * HEAD_DIM)))
    W = bf(np.random.standard_normal((HEAD, NUM_EXPERTS, HEAD_DIM, HEAD_DIM)) / np.sqrt(HEAD_DIM))
    b = bf(np.random.standard_normal(p) * 0.3)
    gamma = bf(np.sqrt(VAR0) * (1.0 + 0.1 * np.random.standard_normal(p)))
    beta = bf(np.random.standard_normal(p) * 0.3)
    running_mean = bf(np.random.standard_normal(p) * 0.3)
    running_var = bf(VAR0 * np.random.uniform(0.5, 1.5, p))
    g = bf(np.random.standard_normal((B, NUM_EXPERTS * HEAD * HEAD_DIM))
           * np.exp2(np.random.randint(-12, 1, (B, 1))) / s)
    y = pre_activation(x10, x20, x30, W, b)
    return {"x1": bf(f64(x10) * s), "x2": bf(f64(x20) * s), "x3": bf(f64(x30) * s),
            "W": W, "b": b, "gamma": gamma, "beta": beta,
            "running_mean": running_mean, "running_var": running_var,
            "y": np.asarray(y, np.float32), "grad_out": g}


def reference(x1, x2, x3, W, b, gamma, beta, running_mean, running_var, y, grad_out):
    n = x1.shape[0]
    xs = np.stack([f64(x1).reshape(n, HEAD, HEAD_DIM),
                   f64(x2).reshape(n, HEAD, HEAD_DIM),
                   f64(x3).reshape(n, HEAD, HEAD_DIM)], axis=2)
    yf = f64(y).reshape(n, NUM_EXPERTS, HEAD, HEAD_DIM)
    g = f64(grad_out).reshape(n, NUM_EXPERTS, HEAD, HEAD_DIM)
    c = (f64(gamma) * (1.0 / np.sqrt(f64(running_var) + EPS))).transpose(1, 0, 2)
    sg = sigmoid(1.702 * yf)
    dy = g * c * (sg * (1.0 + 1.702 * yf * (1.0 - sg)))
    dq = mxq(dy, 0, "e5m2")
    xq = mxq(xs, 0, "e4m3")
    return dq.transpose(2, 1, 3, 0) @ xq.transpose(1, 2, 0, 3)

@@ -1,0 +1,317 @@
+from contextlib import ExitStack
+
+import concourse.mybir as mybir
+from concourse.masks import make_identity
+
+F32 = mybir.dt.float32
+BF16 = mybir.dt.bfloat16
+U32 = mybir.dt.uint32
+U8 = mybir.dt.uint8
+E4M3_X4 = mybir.dt.float8_e4m3fn_x4
+E5M2_X4 = mybir.dt.float8_e5m2_x4
+ACT = mybir.ActivationFunctionType
+ALU = mybir.AluOpType
+
+P = 128
+PACK = 4
+K_PASS = P * PACK
+TOKENS = 1024
+PASSES = TOKENS // K_PASS
+HEADS = 2
+EXPERTS = 3
+DIM = 512
+F_TILES = DIM // P
+RUN = 8
+EPS = 1e-5
+SLOPE = 1.702
+
+FLOPS = 2 * HEADS * EXPERTS * DIM * DIM * TOKENS
+BYTES = (
+    EXPERTS * TOKENS * HEADS * DIM * 2
+    + TOKENS * HEADS * EXPERTS * DIM * (4 + 2)
+    + 2 * HEADS * EXPERTS * DIM * 2
+    + HEADS * EXPERTS * DIM * DIM * 4
+)
+
+
+def by_token(rows):
+    return rows.rearrange("(p j) w -> p j w", j=PACK)
+
+
+def token_major(tile_ap):
+    return tile_ap.rearrange("p j (r i) -> p r j i", i=RUN)
+
+
+def column_major(tile_ap):
+    return tile_ap.rearrange("p (r i) j -> p r j i", i=RUN)
+
+
+def tile_mom_v_kernel(
+    tc, x1, x2, x3, W, b, gamma, beta, running_mean, running_var, y, grad_out, out
+):
+    nc = tc.nc
+    xs = (x1, x2, x3)
+
+    groups = [(e, c) for e in range(EXPERTS) for c in range(PASSES)]
+    chunks = [(e, c, h) for e in range(EXPERTS) for h in range(HEADS) for c in range(PASSES)]
+    n_chunks = len(chunks)
+    last = n_chunks - 1
+    whole = [slice(0, DIM)]
+    tiles_of_128 = [slice(m * P, (m + 1) * P) for m in range(F_TILES)]
+    halves = [slice(n * 256, (n + 1) * 256) for n in range(DIM // 256)]
+
+    with ExitStack() as ctx:
+        const = ctx.enter_context(tc.tile_pool(name="const", bufs=1))
+        y_pool = ctx.enter_context(tc.tile_pool(name="y", bufs=2 * HEADS))
+        gx_pool = ctx.enter_context(tc.tile_pool(name="gx", bufs=3))
+        work = ctx.enter_context(tc.tile_pool(name="work", bufs=3))
+        grouped = ctx.enter_context(tc.tile_pool(name="grouped", bufs=3))
+        quantised = ctx.enter_context(tc.tile_pool(name="quantised", bufs=2))
+        result_pool = ctx.enter_context(tc.tile_pool(name="result", bufs=2 * F_TILES))
+        psum_coef = ctx.enter_context(tc.psum_pool(name="psum_coef", bufs=2 * HEADS))
+        psum_out = ctx.enter_context(tc.psum_pool(name="psum_out", bufs=F_TILES))
+        ctx.enter_context(tc.manual_schedule())
+
+        n_rows = HEADS * EXPERTS * F_TILES
+        var_rows = const.tile([n_rows, P], BF16)
+        nc.sync.dma_start(out=var_rows[:], in_=running_var.rearrange("h e (m p) -> (h e m) p", p=P))
+        gamma_rows = const.tile([n_rows, P], BF16)
+        nc.sync.dma_start(out=gamma_rows[:], in_=gamma.rearrange("h e (m p) -> (h e m) p", p=P))
+        coef_rows = const.tile([P, P], F32)
+        nc.vector.memset(coef_rows[:], 0.0)
+        ident_f32 = const.tile([P, P], F32)
+        make_identity(nc, ident_f32[:])
+
+        def group_of(i):
+            e, c, h = chunks[i]
+            return PASSES * e + c
+
+        y_tiles = {}
+        g_tiles = {}
+        x_tiles = {}
+
+        def load_y(i, pieces):
+            e, c, h = chunks[i]
+            tokens = slice(c * K_PASS, (c + 1) * K_PASS)
+            col0 = (HEADS * e + h) * DIM
+            y_tile = y_pool.tile([P, PACK, DIM], F32)
+            for cols in pieces:
+                nc.sync.dma_start(
+                    out=y_tile[:, :, cols], in_=by_token(y[tokens, col0 + cols.start : col0 + cols.stop])
+                )
+            y_tiles[i] = y_tile
+
+        def new_gx(k):
+            g_tile = gx_pool.tile([P, PACK, HEADS * DIM], BF16)
+            g_tiles[k] = g_tile
+            x_tile = gx_pool.tile([P, PACK, HEADS * DIM], BF16)
+            x_tiles[k] = x_tile
+
+        def load_g(k, cols):
+            e, c = groups[k]
+            tokens = slice(c * K_PASS, (c + 1) * K_PASS)
+            col0 = e * HEADS * DIM
+            nc.sync.dma_start(
+                out=g_tiles[k][:, :, cols], in_=by_token(grad_out[tokens, col0 + cols.start : col0 + cols.stop])
+            )
+
+        def load_x(k, cols):
+            e, c = groups[k]
+            tokens = slice(c * K_PASS, (c + 1) * K_PASS)
+            nc.sync.dma_start(out=x_tiles[k][:, :, cols], in_=by_token(xs[e][tokens, cols]))
+
+        both_heads = slice(0, HEADS * DIM)
+
+        def load_gx(k):
+            new_gx(k)
+            load_g(k, both_heads)
+            load_x(k, both_heads)
+
+        load_y(0, halves)
+        load_y(1, whole)
+        new_gx(0)
+        new_gx(1)
+        for h in range(HEADS):
+            for k in range(PASSES):
+                load_g(k, slice(h * DIM, (h + 1) * DIM))
+                load_x(k, slice(h * DIM, (h + 1) * DIM))
+            load_y(2 + h, whole)
+        load_gx(2)
+
+        std = const.tile([n_rows, P], F32)
+        nc.scalar.activation(out=std[:], in_=var_rows[:], func=ACT.Sqrt, bias=EPS)
+        inv_std = const.tile([n_rows, P], F32)
+        nc.vector.reciprocal(out=inv_std[:], in_=std[:])
+        nc.vector.scalar_tensor_tensor(
+            out=coef_rows[0:n_rows, :], in0=gamma_rows[:], scalar=-0.5, in1=inv_std[:], op0=ALU.mult, op1=ALU.mult
+        )
+
+        coef_all = {}
+        codes = {}
+
+        def start_expert(e):
+            for h in range(HEADS):
+                bank = psum_coef.tile([P, DIM], F32)
+                for m in range(F_TILES):
+                    row = (EXPERTS * h + e) * F_TILES + m
+                    nc.tensor.matmul(
+                        out=bank[:, m * P : (m + 1) * P],
+                        lhsT=ident_f32[:, row : row + 1].to_broadcast([P, P]),
+                        rhs=coef_rows[:],
+                        start=True,
+                        stop=True,
+                    )
+                coef_all[(e, h)] = bank
+            dy_codes = quantised.tile([P, HEADS, PASSES, DIM], U32, align_bytes=64)
+            dy_scales = quantised.tile([P, HEADS, PASSES, DIM], U8, align_bytes=64)
+            x_codes = quantised.tile([P, HEADS, PASSES, DIM], U32, align_bytes=64)
+            x_scales = quantised.tile([P, HEADS, PASSES, DIM], U8, align_bytes=64)
+            codes[e] = (dy_codes, dy_scales, x_codes, x_scales)
+
+        tanh_part = {}
+        silu_part = {}
+        x_grouped = {}
+        dy_grouped = {}
+
+        def functions(i, pieces):
+            e, c, h = chunks[i]
+            if c == 0 and h == 0:
+                start_expert(e)
+            tanh_part[i] = work.tile([P, PACK, DIM], F32, name="tanh_part")
+            silu_part[i] = work.tile([P, PACK, DIM], F32, name="silu_part")
+            for cols in pieces:
+                nc.scalar.activation(
+                    out=tanh_part[i][:, :, cols], in_=y_tiles[i][:, :, cols], func=ACT.Tanh, scale=SLOPE / 2
+                )
+                nc.scalar.activation(
+                    out=silu_part[i][:, :, cols], in_=y_tiles[i][:, :, cols], func=ACT.Silu, scale=-SLOPE
+                )
+
+        def regroup_x(i):
+            e, c, h = chunks[i]
+            x_grouped[i] = grouped.tile([P, DIM, PACK], BF16, name="x_grouped", align_bytes=64)
+            nc.scalar.copy(
+                out=column_major(x_grouped[i][:]),
+                in_=token_major(x_tiles[group_of(i)][:, :, h * DIM : (h + 1) * DIM]),
+            )
+
+        def first_multiply(i, cols):
+            e, c, h = chunks[i]
+            width = cols.stop - cols.start
+            nc.vector.scalar_tensor_tensor(
+                out=tanh_part[i][:, :, cols],
+                in0=tanh_part[i][:, :, cols],
+                scalar=1.0,
+                in1=coef_all[(e, h)][:, cols].unsqueeze(1).to_broadcast([P, PACK, width]),
+                op0=ALU.add,
+                op1=ALU.mult,
+            )
+
+        def second_multiply(i, cols):
+            nc.vector.scalar_tensor_tensor(
+                out=silu_part[i][:, :, cols],
+                in0=silu_part[i][:, :, cols],
+                scalar=1.0,
+                in1=tanh_part[i][:, :, cols],
+                op0=ALU.subtract,
+                op1=ALU.mult,
+            )
+
+        def third_multiply(i, cols):
+            e, c, h = chunks[i]
+            if i not in dy_grouped:
+                dy_grouped[i] = grouped.tile([P, DIM, PACK], BF16, name="dy_grouped", align_bytes=64)
+            nc.vector.tensor_tensor(
+                out=column_major(dy_grouped[i][:, cols, :]),
+                in0=token_major(silu_part[i][:, :, cols]),
+                in1=token_major(g_tiles[group_of(i)][:, :, h * DIM + cols.start : h * DIM + cols.stop]),
+                op=ALU.mult,
+            )
+
+        def quantise_x(i):
+            e, c, h = chunks[i]
+            x_codes, x_scales = codes[e][2:4]
+            nc.vector.quantize_mx(
+                out=x_codes[:, h, c, :].bitcast(E4M3_X4),
+                scales=x_scales[:, h, c, :],
+                in_=x_grouped[i][:].rearrange("p w j -> p (w j)"),
+            )
+
+        def quantise_dy(i, cols):
+            e, c, h = chunks[i]
+            dy_codes, dy_scales = codes[e][0:2]
+            nc.vector.quantize_mx(
+                out=dy_codes[:, h, c, cols].bitcast(E5M2_X4),
+                scales=dy_scales[:, h, c, cols],
+                in_=dy_grouped[i][:, cols, :].rearrange("p w j -> p (w j)"),
+            )
+
+        accs = {}
+
+        def multiply(e, h, m, k):
+            dy_codes, dy_scales, x_codes, x_scales = codes[e]
+            f_cols = tiles_of_128[m]
+            if k == 0:
+                acc = psum_out.tile([P, DIM], F32)
+                accs[(e, h, m)] = acc
+            nc.tensor.matmul_mx(
+                out=accs[(e, h, m)][:],
+                lhsT=dy_codes[:, h, k, f_cols].bitcast(E5M2_X4),
+                lhsT_scale=dy_scales[:, h, k, f_cols],
+                rhs=x_codes[:, h, k, :].bitcast(E4M3_X4),
+                rhs_scale=x_scales[:, h, k, :],
+                start=(k == 0),
+                stop=(k == PASSES - 1),
+            )
+
+        def store(e, h, m):
+            result = result_pool.tile([P, DIM], F32)
+            nc.scalar.copy(out=result[:], in_=accs[(e, h, m)][:])
+            nc.sync.dma_start(out=out[h, e, tiles_of_128[m], :], in_=result[:])
+
+        def finish_chunk(i):
+            e, c, h = chunks[i]
+            quantise_dy(i, whole[0])
+            if c < PASSES - 1:
+                return
+            for m in range(F_TILES):
+                for k in range(PASSES):
+                    multiply(e, h, m, k)
+                store(e, h, m)
+
+        functions(0, halves)
+        functions(1, whole)
+        regroup_x(0)
+        for cols in halves:
+            first_multiply(0, cols)
+            second_multiply(0, cols)
+        for i in range(n_chunks):
+            if i + 2 < n_chunks:
+                functions(i + 2, whole)
+            if i + 1 < n_chunks:
+                regroup_x(i + 1)
+            if i + 4 < n_chunks:
+                load_y(i + 4, whole)
+            if i > 0:
+                second_multiply(i, whole[0])
+            if i + 1 < n_chunks:
+                first_multiply(i + 1, whole[0])
+            if i >= 1:
+                finish_chunk(i - 1)
+            if i < last:
+                third_multiply(i, whole[0])
+                quantise_x(i)
+            next_group = group_of(i) + 3
+            if chunks[i][2] == HEADS - 1 and next_group < len(groups):
+                load_gx(next_group)
+        e, c, h = chunks[last]
+        quantise_x(last)
+        for m in range(F_TILES):
+            multiply(e, h, m, 0)
+        third_multiply(last, tiles_of_128[0])
+        for m in range(F_TILES):
+            if m + 1 < F_TILES:
+                third_multiply(last, tiles_of_128[m + 1])
+            quantise_dy(last, tiles_of_128[m])
+            multiply(e, h, m, 1)
+            store(e, h, m)

@@ -21,6 +21,7 @@ HEADS = 2
 EXPERTS = 3
 DIM = 512
 F_TILES = DIM // P
+G_COLS = 320
 RUN = 8
 EPS = 1e-5
 SLOPE = 1.702
@@ -63,13 +64,16 @@ def tile_mom_v_kernel(
     with ExitStack() as ctx:
         const = ctx.enter_context(tc.tile_pool(name="const", bufs=1))
         y_pool = ctx.enter_context(tc.tile_pool(name="y", bufs=2 * HEADS))
-        gx_pool = ctx.enter_context(tc.tile_pool(name="gx", bufs=3))
+        g_pool = ctx.enter_context(tc.tile_pool(name="g", bufs=3))
+        x_in_pool = ctx.enter_context(tc.tile_pool(name="x_in", bufs=4))
         work = ctx.enter_context(tc.tile_pool(name="work", bufs=3))
-        grouped = ctx.enter_context(tc.tile_pool(name="grouped", bufs=3))
+        x_pool = ctx.enter_context(tc.tile_pool(name="x_grouped", bufs=2))
+        dy_pool = ctx.enter_context(tc.tile_pool(name="dy_grouped", bufs=3))
         quantised = ctx.enter_context(tc.tile_pool(name="quantised", bufs=2))
         result_pool = ctx.enter_context(tc.tile_pool(name="result", bufs=2 * F_TILES))
-        psum_coef = ctx.enter_context(tc.psum_pool(name="psum_coef", bufs=2 * HEADS))
-        psum_out = ctx.enter_context(tc.psum_pool(name="psum_out", bufs=F_TILES))
+        psum_y = ctx.enter_context(tc.psum_pool(name="psum_y", bufs=2))
+        psum_a = ctx.enter_context(tc.psum_pool(name="psum_a", bufs=4))
+        psum_out = ctx.enter_context(tc.psum_pool(name="psum_out", bufs=2))
         ctx.enter_context(tc.manual_schedule())
 
         n_rows = HEADS * EXPERTS * F_TILES
@@ -101,10 +105,12 @@ def tile_mom_v_kernel(
                 )
             y_tiles[i] = y_tile
 
-        def new_gx(k):
-            g_tile = gx_pool.tile([P, PACK, HEADS * DIM], BF16)
+        def new_g(k):
+            g_tile = g_pool.tile([P, PACK, HEADS * DIM], BF16)
             g_tiles[k] = g_tile
-            x_tile = gx_pool.tile([P, PACK, HEADS * DIM], BF16)
+
+        def new_x(k):
+            x_tile = x_in_pool.tile([P, PACK, HEADS * DIM], BF16)
             x_tiles[k] = x_tile
 
         def load_g(k, cols):
@@ -122,21 +128,28 @@ def tile_mom_v_kernel(
 
         both_heads = slice(0, HEADS * DIM)
 
-        def load_gx(k):
-            new_gx(k)
-            load_g(k, both_heads)
-            load_x(k, both_heads)
-
+        head_cols = [slice(h * DIM, (h + 1) * DIM) for h in range(HEADS)]
         load_y(0, halves)
+        for k in range(PASSES):
+            new_x(k)
+            new_g(k)
+        load_x(0, head_cols[0])
         load_y(1, whole)
-        new_gx(0)
-        new_gx(1)
-        for h in range(HEADS):
-            for k in range(PASSES):
-                load_g(k, slice(h * DIM, (h + 1) * DIM))
-                load_x(k, slice(h * DIM, (h + 1) * DIM))
-            load_y(2 + h, whole)
-        load_gx(2)
+        load_x(1, head_cols[0])
+        load_x(0, head_cols[1])
+        load_g(0, head_cols[0])
+        load_y(2, whole)
+        load_g(1, head_cols[0])
+        load_g(0, head_cols[1])
+        load_y(3, whole)
+        load_x(1, head_cols[1])
+        load_g(1, head_cols[1])
+        new_x(2)
+        load_x(2, both_heads)
+        new_g(2)
+        load_g(2, both_heads)
+        new_x(3)
+        load_x(3, both_heads)
 
         std = const.tile([n_rows, P], F32)
         nc.scalar.activation(out=std[:], in_=var_rows[:], func=ACT.Sqrt, bias=EPS)
@@ -145,23 +158,14 @@ def tile_mom_v_kernel(
         nc.vector.scalar_tensor_tensor(
             out=coef_rows[0:n_rows, :], in0=gamma_rows[:], scalar=-0.5, in1=inv_std[:], op0=ALU.mult, op1=ALU.mult
         )
+        coef_bank = psum_a.tile([P, DIM], F32, name="by_tokens")
+        nc.tensor.transpose(coef_bank[:, 0:P], coef_rows[:], ident_f32[:])
+        coef = const.tile([P, n_rows], F32)
+        nc.vector.tensor_copy(out=coef[:], in_=coef_bank[:, 0:n_rows])
 
-        coef_all = {}
         codes = {}
 
         def start_expert(e):
-            for h in range(HEADS):
-                bank = psum_coef.tile([P, DIM], F32)
-                for m in range(F_TILES):
-                    row = (EXPERTS * h + e) * F_TILES + m
-                    nc.tensor.matmul(
-                        out=bank[:, m * P : (m + 1) * P],
-                        lhsT=ident_f32[:, row : row + 1].to_broadcast([P, P]),
-                        rhs=coef_rows[:],
-                        start=True,
-                        stop=True,
-                    )
-                coef_all[(e, h)] = bank
             dy_codes = quantised.tile([P, HEADS, PASSES, DIM], U32, align_bytes=64)
             dy_scales = quantised.tile([P, HEADS, PASSES, DIM], U8, align_bytes=64)
             x_codes = quantised.tile([P, HEADS, PASSES, DIM], U32, align_bytes=64)
@@ -172,47 +176,58 @@ def tile_mom_v_kernel(
         silu_part = {}
         x_grouped = {}
         dy_grouped = {}
+        by_features = {}
+        by_tokens = {}
 
-        def functions(i, pieces):
-            e, c, h = chunks[i]
-            if c == 0 and h == 0:
-                start_expert(e)
-            tanh_part[i] = work.tile([P, PACK, DIM], F32, name="tanh_part")
-            silu_part[i] = work.tile([P, PACK, DIM], F32, name="silu_part")
-            for cols in pieces:
-                nc.scalar.activation(
-                    out=tanh_part[i][:, :, cols], in_=y_tiles[i][:, :, cols], func=ACT.Tanh, scale=SLOPE / 2
-                )
-                nc.scalar.activation(
-                    out=silu_part[i][:, :, cols], in_=y_tiles[i][:, :, cols], func=ACT.Silu, scale=-SLOPE
-                )
+        def turn_y(i, m):
+            bank = psum_y.tile([P, PACK, P], F32, name="by_features")
+            for j in range(PACK):
+                nc.tensor.transpose(bank[:, j, :], y_tiles[i][:, j, tiles_of_128[m]], ident_f32[:])
+            by_features[(i, m)] = bank
 
-        def regroup_x(i):
-            e, c, h = chunks[i]
-            x_grouped[i] = grouped.tile([P, DIM, PACK], BF16, name="x_grouped", align_bytes=64)
-            nc.scalar.copy(
-                out=column_major(x_grouped[i][:]),
-                in_=token_major(x_tiles[group_of(i)][:, :, h * DIM : (h + 1) * DIM]),
+        def tanh(i, m):
+            if m == 0:
+                tanh_part[i] = work.tile([P, F_TILES, PACK * P], F32, name="tanh_part")
+            nc.scalar.activation(
+                out=tanh_part[i][:, m, :],
+                in_=by_features[(i, m)][:].rearrange("f j p -> f (j p)"),
+                func=ACT.Tanh,
+                scale=SLOPE / 2,
             )
 
-        def first_multiply(i, cols):
+        def silu(i, m):
+            cols = tiles_of_128[m]
+            if m == 0:
+                silu_part[i] = work.tile([P, PACK, DIM], F32, name="silu_part")
+            nc.scalar.activation(
+                out=silu_part[i][:, :, cols], in_=y_tiles[i][:, :, cols], func=ACT.Silu, scale=-SLOPE
+            )
+
+        def times_coef(i, m):
             e, c, h = chunks[i]
-            width = cols.stop - cols.start
-            nc.vector.scalar_tensor_tensor(
-                out=tanh_part[i][:, :, cols],
-                in0=tanh_part[i][:, :, cols],
-                scalar=1.0,
-                in1=coef_all[(e, h)][:, cols].unsqueeze(1).to_broadcast([P, PACK, width]),
+            row = (EXPERTS * h + e) * F_TILES + m
+            nc.vector.tensor_scalar(
+                out=tanh_part[i][:, m, :],
+                in0=tanh_part[i][:, m, :],
+                scalar1=1.0,
+                scalar2=coef[:, row : row + 1],
                 op0=ALU.add,
                 op1=ALU.mult,
             )
 
-        def second_multiply(i, cols):
+        def turn_back(i, m):
+            bank = psum_a.tile([P, PACK, P], F32, name="by_tokens")
+            for j in range(PACK):
+                nc.tensor.transpose(bank[:, j, :], tanh_part[i][:, m, j * P : (j + 1) * P], ident_f32[:])
+            by_tokens[(i, m)] = bank
+
+        def second_multiply(i, m):
+            cols = tiles_of_128[m]
             nc.vector.scalar_tensor_tensor(
                 out=silu_part[i][:, :, cols],
                 in0=silu_part[i][:, :, cols],
                 scalar=1.0,
-                in1=tanh_part[i][:, :, cols],
+                in1=by_tokens[(i, m)][:],
                 op0=ALU.subtract,
                 op1=ALU.mult,
             )
@@ -220,7 +235,7 @@ def tile_mom_v_kernel(
         def third_multiply(i, cols):
             e, c, h = chunks[i]
             if i not in dy_grouped:
-                dy_grouped[i] = grouped.tile([P, DIM, PACK], BF16, name="dy_grouped", align_bytes=64)
+                dy_grouped[i] = dy_pool.tile([P, DIM, PACK], BF16, name="dy_grouped", align_bytes=64)
             nc.vector.tensor_tensor(
                 out=column_major(dy_grouped[i][:, cols, :]),
                 in0=token_major(silu_part[i][:, :, cols]),
@@ -228,8 +243,31 @@ def tile_mom_v_kernel(
                 op=ALU.mult,
             )
 
+        def regroup_x(i, cols, copy):
+            e, c, h = chunks[i]
+            copy(
+                out=column_major(x_grouped[i][:, cols, :]),
+                in_=token_major(x_tiles[group_of(i)][:, :, h * DIM + cols.start : h * DIM + cols.stop]),
+            )
+
+        def new_x_grouped(i):
+            x_grouped[i] = x_pool.tile([P, DIM, PACK], BF16, name="x_grouped", align_bytes=64)
+
+        def regroup_x_gpsimd(i, cols):
+            e, c, h = chunks[i]
+            nc.gpsimd.tensor_scalar(
+                out=x_grouped[i][:, cols, :],
+                in0=x_tiles[group_of(i)][:, :, h * DIM + cols.start : h * DIM + cols.stop].rearrange("p j w -> p w j"),
+                scalar1=1.0,
+                scalar2=0.0,
+                op0=ALU.mult,
+                op1=ALU.add,
+            )
+
         def quantise_x(i):
             e, c, h = chunks[i]
+            if c == 0 and h == 0:
+                start_expert(e)
             x_codes, x_scales = codes[e][2:4]
             nc.vector.quantize_mx(
                 out=x_codes[:, h, c, :].bitcast(E4M3_X4),
@@ -246,72 +284,98 @@ def tile_mom_v_kernel(
                 in_=dy_grouped[i][:, cols, :].rearrange("p w j -> p (w j)"),
             )
 
-        accs = {}
-
-        def multiply(e, h, m, k):
+        def finish_tile(i, m):
+            e, c, h = chunks[i]
             dy_codes, dy_scales, x_codes, x_scales = codes[e]
             f_cols = tiles_of_128[m]
-            if k == 0:
-                acc = psum_out.tile([P, DIM], F32)
-                accs[(e, h, m)] = acc
-            nc.tensor.matmul_mx(
-                out=accs[(e, h, m)][:],
-                lhsT=dy_codes[:, h, k, f_cols].bitcast(E5M2_X4),
-                lhsT_scale=dy_scales[:, h, k, f_cols],
-                rhs=x_codes[:, h, k, :].bitcast(E4M3_X4),
-                rhs_scale=x_scales[:, h, k, :],
-                start=(k == 0),
-                stop=(k == PASSES - 1),
-            )
-
-        def store(e, h, m):
+            acc = psum_out.tile([P, DIM], F32)
+            for k in range(PASSES):
+                nc.tensor.matmul_mx(
+                    out=acc[:],
+                    lhsT=dy_codes[:, h, k, f_cols].bitcast(E5M2_X4),
+                    lhsT_scale=dy_scales[:, h, k, f_cols],
+                    rhs=x_codes[:, h, k, :].bitcast(E4M3_X4),
+                    rhs_scale=x_scales[:, h, k, :],
+                    start=(k == 0),
+                    stop=(k == PASSES - 1),
+                )
             result = result_pool.tile([P, DIM], F32)
-            nc.scalar.copy(out=result[:], in_=accs[(e, h, m)][:])
-            nc.sync.dma_start(out=out[h, e, tiles_of_128[m], :], in_=result[:])
+            nc.scalar.copy(out=result[:], in_=acc[:])
+            nc.sync.dma_start(out=out[h, e, f_cols, :], in_=result[:])
 
-        def finish_chunk(i):
-            e, c, h = chunks[i]
-            quantise_dy(i, whole[0])
-            if c < PASSES - 1:
-                return
-            for m in range(F_TILES):
-                for k in range(PASSES):
-                    multiply(e, h, m, k)
-                store(e, h, m)
+        g_share = slice(0, G_COLS)
+        s_share = slice(G_COLS, DIM)
 
-        functions(0, halves)
-        functions(1, whole)
-        regroup_x(0)
-        for cols in halves:
-            first_multiply(0, cols)
-            second_multiply(0, cols)
+        new_x_grouped(0)
+        turn_y(0, 0)
+        turn_y(0, 1)
+        for m in range(F_TILES):
+            tanh(0, m)
+            silu(0, m)
+            times_coef(0, m)
+            if m < 2:
+                turn_y(0, m + 2)
+            else:
+                turn_y(1, m - 2)
+            if m == 1:
+                regroup_x(0, whole[0], nc.vector.tensor_copy)
+        for m in range(F_TILES):
+            turn_back(0, m)
+        load_y(4, whole)
+        new_x_grouped(1)
+        for m in range(F_TILES):
+            tanh(1, m)
+            silu(1, m)
+            if m < 2:
+                turn_y(1, m + 2)
+            else:
+                turn_y(2, m - 2)
+        load_y(5, whole)
         for i in range(n_chunks):
+            quantise_x(i)
             if i + 2 < n_chunks:
-                functions(i + 2, whole)
+                new_x_grouped(i + 2)
+                regroup_x_gpsimd(i + 2, g_share)
+            for m in range(F_TILES):
+                second_multiply(i, m)
+            if i == 0:
+                regroup_x(1, whole[0], nc.vector.tensor_copy)
+            if i >= 2 and chunks[i - 2][1] == PASSES - 1:
+                finish_tile(i - 2, 2)
+                finish_tile(i - 2, 3)
+            if i + 2 < n_chunks:
+                for m in range(F_TILES):
+                    tanh(i + 2, m)
+                    silu(i + 2, m)
+                    if m < 2:
+                        turn_y(i + 2, m + 2)
+            if i + 6 < n_chunks:
+                load_y(i + 6, whole)
             if i + 1 < n_chunks:
-                regroup_x(i + 1)
-            if i + 4 < n_chunks:
-                load_y(i + 4, whole)
-            if i > 0:
-                second_multiply(i, whole[0])
-            if i + 1 < n_chunks:
-                first_multiply(i + 1, whole[0])
+                for m in range(F_TILES):
+                    times_coef(i + 1, m)
+                    turn_back(i + 1, m)
+            if i + 3 < n_chunks:
+                turn_y(i + 3, 0)
+                turn_y(i + 3, 1)
             if i >= 1:
-                finish_chunk(i - 1)
+                quantise_dy(i - 1, whole[0])
+                if chunks[i - 1][1] == PASSES - 1:
+                    finish_tile(i - 1, 0)
+                    finish_tile(i - 1, 1)
             if i < last:
                 third_multiply(i, whole[0])
-                quantise_x(i)
-            next_group = group_of(i) + 3
-            if chunks[i][2] == HEADS - 1 and next_group < len(groups):
-                load_gx(next_group)
-        e, c, h = chunks[last]
-        quantise_x(last)
+            if i + 2 < n_chunks:
+                regroup_x(i + 2, s_share, nc.scalar.copy)
+                next_x = group_of(i + 2) + 4
+                if chunks[i + 2][2] == HEADS - 1 and next_x < len(groups):
+                    new_x(next_x)
+                    load_x(next_x, both_heads)
+            next_g = group_of(i) + 3
+            if chunks[i][2] == HEADS - 1 and next_g < len(groups):
+                new_g(next_g)
+                load_g(next_g, both_heads)
         for m in range(F_TILES):
-            multiply(e, h, m, 0)
-        third_multiply(last, tiles_of_128[0])
-        for m in range(F_TILES):
-            if m + 1 < F_TILES:
-                third_multiply(last, tiles_of_128[m + 1])
+            third_multiply(last, tiles_of_128[m])
             quantise_dy(last, tiles_of_128[m])
-            multiply(e, h, m, 1)
-            store(e, h, m)
+            finish_tile(last, m)

@@ -21,7 +21,8 @@ HEADS = 2
 EXPERTS = 3
 DIM = 512
 F_TILES = DIM // P
-G_COLS = 320
+TURNED = 2
+G_COLS = 352
 RUN = 8
 EPS = 1e-5
 SLOPE = 1.702
@@ -59,7 +60,8 @@ def tile_mom_v_kernel(
     last = n_chunks - 1
     whole = [slice(0, DIM)]
     tiles_of_128 = [slice(m * P, (m + 1) * P) for m in range(F_TILES)]
-    halves = [slice(n * 256, (n + 1) * 256) for n in range(DIM // 256)]
+    turned = slice(0, TURNED * P)
+    straight = slice(TURNED * P, DIM)
 
     with ExitStack() as ctx:
         const = ctx.enter_context(tc.tile_pool(name="const", bufs=1))
@@ -72,7 +74,8 @@ def tile_mom_v_kernel(
         quantised = ctx.enter_context(tc.tile_pool(name="quantised", bufs=2))
         result_pool = ctx.enter_context(tc.tile_pool(name="result", bufs=2 * F_TILES))
         psum_y = ctx.enter_context(tc.psum_pool(name="psum_y", bufs=2))
-        psum_a = ctx.enter_context(tc.psum_pool(name="psum_a", bufs=4))
+        psum_a = ctx.enter_context(tc.psum_pool(name="psum_a", bufs=2))
+        psum_coef = ctx.enter_context(tc.psum_pool(name="psum_coef", bufs=2))
         psum_out = ctx.enter_context(tc.psum_pool(name="psum_out", bufs=2))
         ctx.enter_context(tc.manual_schedule())
 
@@ -129,7 +132,7 @@ def tile_mom_v_kernel(
         both_heads = slice(0, HEADS * DIM)
 
         head_cols = [slice(h * DIM, (h + 1) * DIM) for h in range(HEADS)]
-        load_y(0, halves)
+        load_y(0, [straight, turned])
         for k in range(PASSES):
             new_x(k)
             new_g(k)
@@ -164,15 +167,29 @@ def tile_mom_v_kernel(
         nc.vector.tensor_copy(out=coef[:], in_=coef_bank[:, 0:n_rows])
 
         codes = {}
+        coef_all = {}
 
         def start_expert(e):
+            bank = psum_coef.tile([P, HEADS, F_TILES - TURNED, P], F32, name="coef_all")
+            for h in range(HEADS):
+                for m in range(TURNED, F_TILES):
+                    row = (EXPERTS * h + e) * F_TILES + m
+                    nc.tensor.matmul(
+                        out=bank[:, h, m - TURNED, :],
+                        lhsT=ident_f32[:, row : row + 1].to_broadcast([P, P]),
+                        rhs=coef_rows[:],
+                        start=True,
+                        stop=True,
+                    )
+            coef_all[e] = bank
             dy_codes = quantised.tile([P, HEADS, PASSES, DIM], U32, align_bytes=64)
             dy_scales = quantised.tile([P, HEADS, PASSES, DIM], U8, align_bytes=64)
             x_codes = quantised.tile([P, HEADS, PASSES, DIM], U32, align_bytes=64)
             x_scales = quantised.tile([P, HEADS, PASSES, DIM], U8, align_bytes=64)
             codes[e] = (dy_codes, dy_scales, x_codes, x_scales)
 
-        tanh_part = {}
+        tanh_turned = {}
+        tanh_straight = {}
         silu_part = {}
         x_grouped = {}
         dy_grouped = {}
@@ -185,52 +202,87 @@ def tile_mom_v_kernel(
                 nc.tensor.transpose(bank[:, j, :], y_tiles[i][:, j, tiles_of_128[m]], ident_f32[:])
             by_features[(i, m)] = bank
 
-        def tanh(i, m):
-            if m == 0:
-                tanh_part[i] = work.tile([P, F_TILES, PACK * P], F32, name="tanh_part")
+        def start_chunk(i):
+            e, c, h = chunks[i]
+            tanh_turned[i] = work.tile([P, TURNED, PACK * P], F32, name="tanh_turned")
+            tanh_straight[i] = work.tile([P, PACK, DIM - TURNED * P], F32, name="tanh_straight")
+            silu_part[i] = work.tile([P, PACK, DIM], F32, name="silu_part")
+
+        def take_tanh_turned(i, m):
             nc.scalar.activation(
-                out=tanh_part[i][:, m, :],
+                out=tanh_turned[i][:, m, :],
                 in_=by_features[(i, m)][:].rearrange("f j p -> f (j p)"),
                 func=ACT.Tanh,
                 scale=SLOPE / 2,
             )
 
-        def silu(i, m):
-            cols = tiles_of_128[m]
-            if m == 0:
-                silu_part[i] = work.tile([P, PACK, DIM], F32, name="silu_part")
+        def take_tanh_straight(i):
+            nc.scalar.activation(
+                out=tanh_straight[i][:], in_=y_tiles[i][:, :, straight], func=ACT.Tanh, scale=SLOPE / 2
+            )
+
+        def take_silu(i, cols):
             nc.scalar.activation(
                 out=silu_part[i][:, :, cols], in_=y_tiles[i][:, :, cols], func=ACT.Silu, scale=-SLOPE
             )
 
-        def times_coef(i, m):
+        def coef_column(i, m):
             e, c, h = chunks[i]
             row = (EXPERTS * h + e) * F_TILES + m
+            return coef[:, row : row + 1]
+
+        def times_coef_vector(i, m):
             nc.vector.tensor_scalar(
-                out=tanh_part[i][:, m, :],
-                in0=tanh_part[i][:, m, :],
+                out=tanh_turned[i][:, m, :],
+                in0=tanh_turned[i][:, m, :],
                 scalar1=1.0,
-                scalar2=coef[:, row : row + 1],
+                scalar2=coef_column(i, m),
                 op0=ALU.add,
                 op1=ALU.mult,
+            )
+
+        def times_coef_scalar(i, m):
+            nc.scalar.activation(
+                out=tanh_turned[i][:, m, :],
+                in_=tanh_turned[i][:, m, :],
+                func=ACT.Identity,
+                scale=coef_column(i, m),
+                bias=coef_column(i, m),
             )
 
         def turn_back(i, m):
             bank = psum_a.tile([P, PACK, P], F32, name="by_tokens")
             for j in range(PACK):
-                nc.tensor.transpose(bank[:, j, :], tanh_part[i][:, m, j * P : (j + 1) * P], ident_f32[:])
+                nc.tensor.transpose(bank[:, j, :], tanh_turned[i][:, m, j * P : (j + 1) * P], ident_f32[:])
             by_tokens[(i, m)] = bank
 
-        def second_multiply(i, m):
-            cols = tiles_of_128[m]
+        def first_multiply_straight(i):
+            e, c, h = chunks[i]
+            row_coef = coef_all[e][:, h, :, :].rearrange("p m f -> p (m f)")
+            nc.vector.scalar_tensor_tensor(
+                out=tanh_straight[i][:],
+                in0=tanh_straight[i][:],
+                scalar=1.0,
+                in1=row_coef.unsqueeze(1).to_broadcast([P, PACK, DIM - TURNED * P]),
+                op0=ALU.add,
+                op1=ALU.mult,
+            )
+
+        def second_multiply(i, cols, factor):
             nc.vector.scalar_tensor_tensor(
                 out=silu_part[i][:, :, cols],
                 in0=silu_part[i][:, :, cols],
                 scalar=1.0,
-                in1=by_tokens[(i, m)][:],
+                in1=factor[:],
                 op0=ALU.subtract,
                 op1=ALU.mult,
             )
+
+        def second_multiply_turned(i, m):
+            second_multiply(i, tiles_of_128[m], by_tokens[(i, m)])
+
+        def second_multiply_straight(i):
+            second_multiply(i, straight, tanh_straight[i])
 
         def third_multiply(i, cols):
             e, c, h = chunks[i]
@@ -266,8 +318,6 @@ def tile_mom_v_kernel(
 
         def quantise_x(i):
             e, c, h = chunks[i]
-            if c == 0 and h == 0:
-                start_expert(e)
             x_codes, x_scales = codes[e][2:4]
             nc.vector.quantize_mx(
                 out=x_codes[:, h, c, :].bitcast(E4M3_X4),
@@ -306,58 +356,68 @@ def tile_mom_v_kernel(
         g_share = slice(0, G_COLS)
         s_share = slice(G_COLS, DIM)
 
+        start_expert(0)
         new_x_grouped(0)
-        turn_y(0, 0)
-        turn_y(0, 1)
-        for m in range(F_TILES):
-            tanh(0, m)
-            silu(0, m)
-            times_coef(0, m)
-            if m < 2:
-                turn_y(0, m + 2)
-            else:
-                turn_y(1, m - 2)
-            if m == 1:
-                regroup_x(0, whole[0], nc.vector.tensor_copy)
-        for m in range(F_TILES):
-            turn_back(0, m)
-        load_y(4, whole)
         new_x_grouped(1)
-        for m in range(F_TILES):
-            tanh(1, m)
-            silu(1, m)
-            if m < 2:
-                turn_y(1, m + 2)
-            else:
-                turn_y(2, m - 2)
+        start_chunk(0)
+        take_tanh_straight(0)
+        first_multiply_straight(0)
+        take_silu(0, straight)
+        for m in range(TURNED):
+            turn_y(0, m)
+        second_multiply_straight(0)
+        for m in range(TURNED):
+            take_tanh_turned(0, m)
+            turn_y(1, m)
+        times_coef_vector(0, 0)
+        times_coef_scalar(0, 1)
+        for m in range(TURNED):
+            turn_back(0, m)
+        take_silu(0, turned)
+        regroup_x(0, whole[0], nc.vector.tensor_copy)
+        load_y(4, whole)
+        start_chunk(1)
+        take_tanh_straight(1)
+        for m in range(TURNED):
+            take_tanh_turned(1, m)
+            turn_y(2, m)
+        times_coef_scalar(1, 1)
+        take_silu(1, whole[0])
         load_y(5, whole)
         for i in range(n_chunks):
             quantise_x(i)
             if i + 2 < n_chunks:
                 new_x_grouped(i + 2)
                 regroup_x_gpsimd(i + 2, g_share)
-            for m in range(F_TILES):
-                second_multiply(i, m)
+            for m in range(TURNED):
+                second_multiply_turned(i, m)
+            if i + 1 < n_chunks:
+                first_multiply_straight(i + 1)
             if i == 0:
                 regroup_x(1, whole[0], nc.vector.tensor_copy)
             if i >= 2 and chunks[i - 2][1] == PASSES - 1:
                 finish_tile(i - 2, 2)
                 finish_tile(i - 2, 3)
             if i + 2 < n_chunks:
-                for m in range(F_TILES):
-                    tanh(i + 2, m)
-                    silu(i + 2, m)
-                    if m < 2:
-                        turn_y(i + 2, m + 2)
+                start_chunk(i + 2)
+                if chunks[i + 2][1:] == (0, 0):
+                    start_expert(chunks[i + 2][0])
+                take_tanh_straight(i + 2)
+                for m in range(TURNED):
+                    take_tanh_turned(i + 2, m)
+                times_coef_scalar(i + 2, 1)
+                take_silu(i + 2, whole[0])
             if i + 6 < n_chunks:
                 load_y(i + 6, whole)
             if i + 1 < n_chunks:
-                for m in range(F_TILES):
-                    times_coef(i + 1, m)
+                times_coef_vector(i + 1, 0)
+                for m in range(TURNED):
                     turn_back(i + 1, m)
             if i + 3 < n_chunks:
-                turn_y(i + 3, 0)
-                turn_y(i + 3, 1)
+                for m in range(TURNED):
+                    turn_y(i + 3, m)
+            if i > 0:
+                second_multiply_straight(i)
             if i >= 1:
                 quantise_dy(i - 1, whole[0])
                 if chunks[i - 1][1] == PASSES - 1:

@@ -169,19 +169,19 @@ def tile_mom_v_kernel(
         codes = {}
         coef_all = {}
 
+        def spread_coef(e, h, m):
+            if (h, m) == (0, TURNED):
+                coef_all[e] = psum_coef.tile([P, HEADS, F_TILES - TURNED, P], F32, name="coef_all")
+            row = (EXPERTS * h + e) * F_TILES + m
+            nc.tensor.matmul(
+                out=coef_all[e][:, h, m - TURNED, :],
+                lhsT=ident_f32[:, row : row + 1].to_broadcast([P, P]),
+                rhs=coef_rows[:],
+                start=True,
+                stop=True,
+            )
+
         def start_expert(e):
-            bank = psum_coef.tile([P, HEADS, F_TILES - TURNED, P], F32, name="coef_all")
-            for h in range(HEADS):
-                for m in range(TURNED, F_TILES):
-                    row = (EXPERTS * h + e) * F_TILES + m
-                    nc.tensor.matmul(
-                        out=bank[:, h, m - TURNED, :],
-                        lhsT=ident_f32[:, row : row + 1].to_broadcast([P, P]),
-                        rhs=coef_rows[:],
-                        start=True,
-                        stop=True,
-                    )
-            coef_all[e] = bank
             dy_codes = quantised.tile([P, HEADS, PASSES, DIM], U32, align_bytes=64)
             dy_scales = quantised.tile([P, HEADS, PASSES, DIM], U8, align_bytes=64)
             x_codes = quantised.tile([P, HEADS, PASSES, DIM], U32, align_bytes=64)
@@ -334,7 +334,9 @@ def tile_mom_v_kernel(
                 in_=dy_grouped[i][:, cols, :].rearrange("p w j -> p (w j)"),
             )
 
-        def finish_tile(i, m):
+        accs = {}
+
+        def multiply(i, m):
             e, c, h = chunks[i]
             dy_codes, dy_scales, x_codes, x_scales = codes[e]
             f_cols = tiles_of_128[m]
@@ -349,13 +351,24 @@ def tile_mom_v_kernel(
                     start=(k == 0),
                     stop=(k == PASSES - 1),
                 )
+            accs[(i, m)] = acc
+
+        def store(i, m):
+            e, c, h = chunks[i]
             result = result_pool.tile([P, DIM], F32)
-            nc.scalar.copy(out=result[:], in_=acc[:])
-            nc.sync.dma_start(out=out[h, e, f_cols, :], in_=result[:])
+            nc.scalar.copy(out=result[:], in_=accs[(i, m)][:])
+            nc.sync.dma_start(out=out[h, e, tiles_of_128[m], :], in_=result[:])
+
+        def pair_done(i):
+            return i >= 0 and chunks[i][1] == PASSES - 1
 
         g_share = slice(0, G_COLS)
         s_share = slice(G_COLS, DIM)
 
+        spread_order = [(e, h, m) for e in range(EXPERTS) for h in range(HEADS) for m in range(TURNED, F_TILES)]
+        per_expert = HEADS * (F_TILES - TURNED)
+        for k in range(per_expert // HEADS):
+            spread_coef(*spread_order[k])
         start_expert(0)
         new_x_grouped(0)
         new_x_grouped(1)
@@ -373,6 +386,8 @@ def tile_mom_v_kernel(
         times_coef_scalar(0, 1)
         for m in range(TURNED):
             turn_back(0, m)
+        for k in range(per_expert // HEADS, 2 * per_expert):
+            spread_coef(*spread_order[k])
         take_silu(0, turned)
         regroup_x(0, whole[0], nc.vector.tensor_copy)
         load_y(4, whole)
@@ -395,16 +410,13 @@ def tile_mom_v_kernel(
                 first_multiply_straight(i + 1)
             if i == 0:
                 regroup_x(1, whole[0], nc.vector.tensor_copy)
-            if i >= 2 and chunks[i - 2][1] == PASSES - 1:
-                finish_tile(i - 2, 2)
-                finish_tile(i - 2, 3)
             if i + 2 < n_chunks:
                 start_chunk(i + 2)
                 if chunks[i + 2][1:] == (0, 0):
                     start_expert(chunks[i + 2][0])
-                take_tanh_straight(i + 2)
                 for m in range(TURNED):
                     take_tanh_turned(i + 2, m)
+                take_tanh_straight(i + 2)
                 times_coef_scalar(i + 2, 1)
                 take_silu(i + 2, whole[0])
             if i + 6 < n_chunks:
@@ -420,11 +432,22 @@ def tile_mom_v_kernel(
                 second_multiply_straight(i)
             if i >= 1:
                 quantise_dy(i - 1, whole[0])
-                if chunks[i - 1][1] == PASSES - 1:
-                    finish_tile(i - 1, 0)
-                    finish_tile(i - 1, 1)
+            if pair_done(i - 2):
+                store(i - 2, 0)
+                store(i - 2, 1)
+                multiply(i - 2, 2)
+                multiply(i - 2, 3)
+            if pair_done(i - 3):
+                store(i - 3, 2)
+                store(i - 3, 3)
+            if pair_done(i - 1):
+                multiply(i - 1, 0)
+                multiply(i - 1, 1)
             if i < last:
                 third_multiply(i, whole[0])
+            k = 2 * per_expert + i - 4
+            if i >= 4 and k < 3 * per_expert:
+                spread_coef(*spread_order[k])
             if i + 2 < n_chunks:
                 regroup_x(i + 2, s_share, nc.scalar.copy)
                 next_x = group_of(i + 2) + 4
@@ -438,4 +461,8 @@ def tile_mom_v_kernel(
         for m in range(F_TILES):
             third_multiply(last, tiles_of_128[m])
             quantise_dy(last, tiles_of_128[m])
-            finish_tile(last, m)
+            if m == 0:
+                store(last - 2, 2)
+                store(last - 2, 3)
+            multiply(last, m)
+            store(last, m)

@@ -132,27 +132,19 @@ def tile_mom_v_kernel(
         both_heads = slice(0, HEADS * DIM)
 
         head_cols = [slice(h * DIM, (h + 1) * DIM) for h in range(HEADS)]
-        load_y(0, [straight, turned])
         for k in range(PASSES):
             new_x(k)
             new_g(k)
+        load_y(0, [straight, turned])
         load_x(0, head_cols[0])
         load_y(1, whole)
         load_x(1, head_cols[0])
         load_x(0, head_cols[1])
-        load_g(0, head_cols[0])
         load_y(2, whole)
-        load_g(1, head_cols[0])
-        load_g(0, head_cols[1])
+        load_g(0, head_cols[0])
         load_y(3, whole)
         load_x(1, head_cols[1])
-        load_g(1, head_cols[1])
-        new_x(2)
-        load_x(2, both_heads)
-        new_g(2)
-        load_g(2, both_heads)
-        new_x(3)
-        load_x(3, both_heads)
+        load_g(1, head_cols[0])
 
         std = const.tile([n_rows, P], F32)
         nc.scalar.activation(out=std[:], in_=var_rows[:], func=ACT.Sqrt, bias=EPS)
@@ -386,11 +378,14 @@ def tile_mom_v_kernel(
         times_coef_scalar(0, 1)
         for m in range(TURNED):
             turn_back(0, m)
-        for k in range(per_expert // HEADS, 2 * per_expert):
+        for k in range(per_expert // HEADS, per_expert + 1):
             spread_coef(*spread_order[k])
         take_silu(0, turned)
         regroup_x(0, whole[0], nc.vector.tensor_copy)
         load_y(4, whole)
+        new_x(2)
+        load_x(2, both_heads)
+        load_g(0, head_cols[1])
         start_chunk(1)
         take_tanh_straight(1)
         for m in range(TURNED):
@@ -399,6 +394,7 @@ def tile_mom_v_kernel(
         times_coef_scalar(1, 1)
         take_silu(1, whole[0])
         load_y(5, whole)
+        load_g(1, head_cols[1])
         for i in range(n_chunks):
             quantise_x(i)
             if i + 2 < n_chunks:
@@ -419,6 +415,9 @@ def tile_mom_v_kernel(
                 take_tanh_straight(i + 2)
                 times_coef_scalar(i + 2, 1)
                 take_silu(i + 2, whole[0])
+            if i + 5 < n_chunks and chunks[i + 5][2] == 0:
+                new_x(group_of(i + 5))
+                load_x(group_of(i + 5), both_heads)
             if i + 6 < n_chunks:
                 load_y(i + 6, whole)
             if i + 1 < n_chunks:
@@ -445,19 +444,13 @@ def tile_mom_v_kernel(
                 multiply(i - 1, 1)
             if i < last:
                 third_multiply(i, whole[0])
-            k = 2 * per_expert + i - 4
-            if i >= 4 and k < 3 * per_expert:
-                spread_coef(*spread_order[k])
+            if per_expert + 1 + i < len(spread_order):
+                spread_coef(*spread_order[per_expert + 1 + i])
             if i + 2 < n_chunks:
                 regroup_x(i + 2, s_share, nc.scalar.copy)
-                next_x = group_of(i + 2) + 4
-                if chunks[i + 2][2] == HEADS - 1 and next_x < len(groups):
-                    new_x(next_x)
-                    load_x(next_x, both_heads)
-            next_g = group_of(i) + 3
-            if chunks[i][2] == HEADS - 1 and next_g < len(groups):
-                new_g(next_g)
-                load_g(next_g, both_heads)
+            if i + 3 < n_chunks and group_of(i + 3) >= PASSES and chunks[i + 3][2] == 0:
+                new_g(group_of(i + 3))
+                load_g(group_of(i + 3), both_heads)
         for m in range(F_TILES):
             third_multiply(last, tiles_of_128[m])
             quantise_dy(last, tiles_of_128[m])

@@ -55,7 +55,8 @@ def tile_mom_v_kernel(
     xs = (x1, x2, x3)
 
     groups = [(e, c) for e in range(EXPERTS) for c in range(PASSES)]
-    chunks = [(e, c, h) for e in range(EXPERTS) for h in range(HEADS) for c in range(PASSES)]
+    chunks = [(e, c, h) for e in range(EXPERTS - 1) for c in range(PASSES) for h in range(HEADS)]
+    chunks += [(EXPERTS - 1, c, h) for h in range(HEADS) for c in range(PASSES)]
     n_chunks = len(chunks)
     last = n_chunks - 1
     whole = [slice(0, DIM)]
@@ -65,9 +66,9 @@ def tile_mom_v_kernel(
 
     with ExitStack() as ctx:
         const = ctx.enter_context(tc.tile_pool(name="const", bufs=1))
-        y_pool = ctx.enter_context(tc.tile_pool(name="y", bufs=2 * HEADS))
+        y_pool = ctx.enter_context(tc.tile_pool(name="y", bufs=3))
         g_pool = ctx.enter_context(tc.tile_pool(name="g", bufs=3))
-        x_in_pool = ctx.enter_context(tc.tile_pool(name="x_in", bufs=4))
+        x_in_pool = ctx.enter_context(tc.tile_pool(name="x_in", bufs=3))
         work = ctx.enter_context(tc.tile_pool(name="work", bufs=3))
         x_pool = ctx.enter_context(tc.tile_pool(name="x_grouped", bufs=2))
         dy_pool = ctx.enter_context(tc.tile_pool(name="dy_grouped", bufs=3))
@@ -81,9 +82,16 @@ def tile_mom_v_kernel(
 
         n_rows = HEADS * EXPERTS * F_TILES
         var_rows = const.tile([n_rows, P], BF16)
-        nc.sync.dma_start(out=var_rows[:], in_=running_var.rearrange("h e (m p) -> (h e m) p", p=P))
+        row_blocks = [slice(0, 16), slice(16, n_rows)]
+        for rows in row_blocks:
+            nc.sync.dma_start(
+                out=var_rows[rows, :], in_=running_var.rearrange("h e (m p) -> (h e m) p", p=P)[rows, :]
+            )
         gamma_rows = const.tile([n_rows, P], BF16)
-        nc.sync.dma_start(out=gamma_rows[:], in_=gamma.rearrange("h e (m p) -> (h e m) p", p=P))
+        for rows in row_blocks:
+            nc.sync.dma_start(
+                out=gamma_rows[rows, :], in_=gamma.rearrange("h e (m p) -> (h e m) p", p=P)[rows, :]
+            )
         coef_rows = const.tile([P, P], F32)
         nc.vector.memset(coef_rows[:], 0.0)
         ident_f32 = const.tile([P, P], F32)
@@ -93,20 +101,30 @@ def tile_mom_v_kernel(
             e, c, h = chunks[i]
             return PASSES * e + c
 
+        first_use = {}
+        for i in range(n_chunks):
+            if chunks[i][2] == 0:
+                first_use[i] = group_of(i)
+
         y_tiles = {}
         g_tiles = {}
         x_tiles = {}
 
-        def load_y(i, pieces):
-            e, c, h = chunks[i]
+        def new_y(k):
+            y_tile = y_pool.tile([P, PACK, HEADS * DIM], F32)
+            y_tiles[k] = y_tile
+
+        def load_y(k, cols):
+            e, c = groups[k]
             tokens = slice(c * K_PASS, (c + 1) * K_PASS)
-            col0 = (HEADS * e + h) * DIM
-            y_tile = y_pool.tile([P, PACK, DIM], F32)
-            for cols in pieces:
-                nc.sync.dma_start(
-                    out=y_tile[:, :, cols], in_=by_token(y[tokens, col0 + cols.start : col0 + cols.stop])
-                )
-            y_tiles[i] = y_tile
+            col0 = e * HEADS * DIM
+            nc.sync.dma_start(
+                out=y_tiles[k][:, :, cols], in_=by_token(y[tokens, col0 + cols.start : col0 + cols.stop])
+            )
+
+        def y_columns(i, cols):
+            h = chunks[i][2]
+            return y_tiles[group_of(i)][:, :, h * DIM + cols.start : h * DIM + cols.stop]
 
         def new_g(k):
             g_tile = g_pool.tile([P, PACK, HEADS * DIM], BF16)
@@ -133,19 +151,22 @@ def tile_mom_v_kernel(
 
         head_cols = [slice(h * DIM, (h + 1) * DIM) for h in range(HEADS)]
         for k in range(PASSES):
+            new_y(k)
             new_x(k)
             new_g(k)
-        load_y(0, [straight, turned])
+        load_y(0, straight)
+        load_y(0, turned)
         load_x(0, head_cols[0])
-        load_y(1, whole)
-        load_x(1, head_cols[0])
-        load_x(0, head_cols[1])
-        load_y(2, whole)
+        load_y(0, head_cols[1])
         load_g(0, head_cols[0])
-        load_y(3, whole)
-        load_x(1, head_cols[1])
-        load_g(1, head_cols[0])
+        load_x(0, head_cols[1])
+        load_y(1, head_cols[0])
+        load_x(1, both_heads)
+        load_g(0, head_cols[1])
+        load_y(1, head_cols[1])
 
+        first_sqrt = const.tile([P, 1], F32)
+        nc.scalar.activation(out=first_sqrt[:], in_=coef_rows[:, 0:1], func=ACT.Sqrt)
         std = const.tile([n_rows, P], F32)
         nc.scalar.activation(out=std[:], in_=var_rows[:], func=ACT.Sqrt, bias=EPS)
         inv_std = const.tile([n_rows, P], F32)
@@ -191,7 +212,7 @@ def tile_mom_v_kernel(
         def turn_y(i, m):
             bank = psum_y.tile([P, PACK, P], F32, name="by_features")
             for j in range(PACK):
-                nc.tensor.transpose(bank[:, j, :], y_tiles[i][:, j, tiles_of_128[m]], ident_f32[:])
+                nc.tensor.transpose(bank[:, j, :], y_columns(i, tiles_of_128[m])[:, j, :], ident_f32[:])
             by_features[(i, m)] = bank
 
         def start_chunk(i):
@@ -210,12 +231,12 @@ def tile_mom_v_kernel(
 
         def take_tanh_straight(i):
             nc.scalar.activation(
-                out=tanh_straight[i][:], in_=y_tiles[i][:, :, straight], func=ACT.Tanh, scale=SLOPE / 2
+                out=tanh_straight[i][:], in_=y_columns(i, straight), func=ACT.Tanh, scale=SLOPE / 2
             )
 
         def take_silu(i, cols):
             nc.scalar.activation(
-                out=silu_part[i][:, :, cols], in_=y_tiles[i][:, :, cols], func=ACT.Silu, scale=-SLOPE
+                out=silu_part[i][:, :, cols], in_=y_columns(i, cols), func=ACT.Silu, scale=-SLOPE
             )
 
         def coef_column(i, m):
@@ -359,11 +380,10 @@ def tile_mom_v_kernel(
 
         spread_order = [(e, h, m) for e in range(EXPERTS) for h in range(HEADS) for m in range(TURNED, F_TILES)]
         per_expert = HEADS * (F_TILES - TURNED)
-        for k in range(per_expert // HEADS):
+        for k in range(per_expert):
             spread_coef(*spread_order[k])
         start_expert(0)
         new_x_grouped(0)
-        new_x_grouped(1)
         start_chunk(0)
         take_tanh_straight(0)
         first_multiply_straight(0)
@@ -374,18 +394,16 @@ def tile_mom_v_kernel(
         for m in range(TURNED):
             take_tanh_turned(0, m)
             turn_y(1, m)
-        times_coef_vector(0, 0)
-        times_coef_scalar(0, 1)
         for m in range(TURNED):
+            times_coef_vector(0, m)
             turn_back(0, m)
-        for k in range(per_expert // HEADS, per_expert + 1):
-            spread_coef(*spread_order[k])
+        spread_coef(*spread_order[per_expert])
         take_silu(0, turned)
         regroup_x(0, whole[0], nc.vector.tensor_copy)
-        load_y(4, whole)
-        new_x(2)
-        load_x(2, both_heads)
-        load_g(0, head_cols[1])
+        new_y(2)
+        load_y(2, head_cols[0])
+        load_g(1, both_heads)
+        load_y(2, head_cols[1])
         start_chunk(1)
         take_tanh_straight(1)
         for m in range(TURNED):
@@ -393,19 +411,18 @@ def tile_mom_v_kernel(
             turn_y(2, m)
         times_coef_scalar(1, 1)
         take_silu(1, whole[0])
-        load_y(5, whole)
-        load_g(1, head_cols[1])
+        in_flight = []
+        waiting = []
         for i in range(n_chunks):
-            quantise_x(i)
-            if i + 2 < n_chunks:
-                new_x_grouped(i + 2)
-                regroup_x_gpsimd(i + 2, g_share)
+            if i > 0:
+                quantise_x(i - 1)
+            if i + 1 < n_chunks:
+                new_x_grouped(i + 1)
+                regroup_x_gpsimd(i + 1, g_share)
             for m in range(TURNED):
                 second_multiply_turned(i, m)
             if i + 1 < n_chunks:
                 first_multiply_straight(i + 1)
-            if i == 0:
-                regroup_x(1, whole[0], nc.vector.tensor_copy)
             if i + 2 < n_chunks:
                 start_chunk(i + 2)
                 if chunks[i + 2][1:] == (0, 0):
@@ -415,11 +432,12 @@ def tile_mom_v_kernel(
                 take_tanh_straight(i + 2)
                 times_coef_scalar(i + 2, 1)
                 take_silu(i + 2, whole[0])
-            if i + 5 < n_chunks and chunks[i + 5][2] == 0:
-                new_x(group_of(i + 5))
-                load_x(group_of(i + 5), both_heads)
-            if i + 6 < n_chunks:
-                load_y(i + 6, whole)
+            if i + 4 in first_use:
+                new_x(first_use[i + 4])
+                load_x(first_use[i + 4], both_heads)
+            if i + 6 in first_use:
+                new_y(first_use[i + 6])
+                load_y(first_use[i + 6], both_heads)
             if i + 1 < n_chunks:
                 times_coef_vector(i + 1, 0)
                 for m in range(TURNED):
@@ -431,31 +449,31 @@ def tile_mom_v_kernel(
                 second_multiply_straight(i)
             if i >= 1:
                 quantise_dy(i - 1, whole[0])
-            if pair_done(i - 2):
-                store(i - 2, 0)
-                store(i - 2, 1)
-                multiply(i - 2, 2)
-                multiply(i - 2, 3)
-            if pair_done(i - 3):
-                store(i - 3, 2)
-                store(i - 3, 3)
             if pair_done(i - 1):
-                multiply(i - 1, 0)
-                multiply(i - 1, 1)
+                waiting += [(i - 1, m) for m in range(F_TILES)]
+            for turn in range(1 + (len(waiting) > F_TILES)):
+                for tile in in_flight:
+                    store(*tile)
+                in_flight = waiting[:2]
+                waiting = waiting[2:]
+                for tile in in_flight:
+                    multiply(*tile)
             if i < last:
                 third_multiply(i, whole[0])
+            else:
+                quantise_x(i)
             if per_expert + 1 + i < len(spread_order):
                 spread_coef(*spread_order[per_expert + 1 + i])
-            if i + 2 < n_chunks:
-                regroup_x(i + 2, s_share, nc.scalar.copy)
-            if i + 3 < n_chunks and group_of(i + 3) >= PASSES and chunks[i + 3][2] == 0:
-                new_g(group_of(i + 3))
-                load_g(group_of(i + 3), both_heads)
+            if i + 1 < n_chunks:
+                regroup_x(i + 1, s_share, nc.scalar.copy)
+            if i + 3 in first_use and first_use[i + 3] >= PASSES:
+                new_g(first_use[i + 3])
+                load_g(first_use[i + 3], both_heads)
         for m in range(F_TILES):
             third_multiply(last, tiles_of_128[m])
             quantise_dy(last, tiles_of_128[m])
             if m == 0:
-                store(last - 2, 2)
-                store(last - 2, 3)
+                for tile in in_flight:
+                    store(*tile)
             multiply(last, m)
             store(last, m)

@@ -22,9 +22,10 @@ EXPERTS = 3
 DIM = 512
 F_TILES = DIM // P
 TURNED = 2
-G_COLS = 352
+G_COLS = 384
 RUN = 8
 EPS = 1e-5
+SCALED = (0, 2, 2)
 SLOPE = 1.702
 
 FLOPS = 2 * HEADS * EXPERTS * DIM * DIM * TOKENS
@@ -158,12 +159,13 @@ def tile_mom_v_kernel(
         load_y(0, turned)
         load_x(0, head_cols[0])
         load_y(0, head_cols[1])
-        load_g(0, head_cols[0])
         load_x(0, head_cols[1])
+        load_g(0, head_cols[0])
         load_y(1, head_cols[0])
-        load_x(1, both_heads)
+        load_x(1, head_cols[0])
         load_g(0, head_cols[1])
         load_y(1, head_cols[1])
+        load_x(1, head_cols[1])
 
         first_sqrt = const.tile([P, 1], F32)
         nc.scalar.activation(out=first_sqrt[:], in_=coef_rows[:, 0:1], func=ACT.Sqrt)
@@ -393,10 +395,11 @@ def tile_mom_v_kernel(
         second_multiply_straight(0)
         for m in range(TURNED):
             take_tanh_turned(0, m)
-            turn_y(1, m)
         for m in range(TURNED):
             times_coef_vector(0, m)
             turn_back(0, m)
+        for m in range(TURNED):
+            turn_y(1, m)
         spread_coef(*spread_order[per_expert])
         take_silu(0, turned)
         regroup_x(0, whole[0], nc.vector.tensor_copy)
@@ -409,7 +412,8 @@ def tile_mom_v_kernel(
         for m in range(TURNED):
             take_tanh_turned(1, m)
             turn_y(2, m)
-        times_coef_scalar(1, 1)
+        for m in range(TURNED - SCALED[0], TURNED):
+            times_coef_scalar(1, m)
         take_silu(1, whole[0])
         in_flight = []
         waiting = []
@@ -430,7 +434,8 @@ def tile_mom_v_kernel(
                 for m in range(TURNED):
                     take_tanh_turned(i + 2, m)
                 take_tanh_straight(i + 2)
-                times_coef_scalar(i + 2, 1)
+                for m in range(TURNED - SCALED[chunks[i + 2][0]], TURNED):
+                    times_coef_scalar(i + 2, m)
                 take_silu(i + 2, whole[0])
             if i + 4 in first_use:
                 new_x(first_use[i + 4])
@@ -439,7 +444,8 @@ def tile_mom_v_kernel(
                 new_y(first_use[i + 6])
                 load_y(first_use[i + 6], both_heads)
             if i + 1 < n_chunks:
-                times_coef_vector(i + 1, 0)
+                for m in range(TURNED - SCALED[chunks[i + 1][0]]):
+                    times_coef_vector(i + 1, m)
                 for m in range(TURNED):
                     turn_back(i + 1, m)
             if i + 3 < n_chunks:
@@ -469,11 +475,10 @@ def tile_mom_v_kernel(
             if i + 3 in first_use and first_use[i + 3] >= PASSES:
                 new_g(first_use[i + 3])
                 load_g(first_use[i + 3], both_heads)
+        for tile in in_flight:
+            store(*tile)
         for m in range(F_TILES):
             third_multiply(last, tiles_of_128[m])
             quantise_dy(last, tiles_of_128[m])
-            if m == 0:
-                for tile in in_flight:
-                    store(*tile)
             multiply(last, m)
             store(last, m)

from contextlib import ExitStack

import concourse.mybir as mybir
from concourse.masks import make_identity

F32 = mybir.dt.float32
BF16 = mybir.dt.bfloat16
U32 = mybir.dt.uint32
U8 = mybir.dt.uint8
E4M3_X4 = mybir.dt.float8_e4m3fn_x4
E5M2_X4 = mybir.dt.float8_e5m2_x4
ACT = mybir.ActivationFunctionType
ALU = mybir.AluOpType

P = 128
PACK = 4
K_PASS = P * PACK
TOKENS = 1024
PASSES = TOKENS // K_PASS
HEADS = 2
EXPERTS = 3
DIM = 512
F_TILES = DIM // P
TURNED = 2
G_COLS = 384
RUN = 8
EPS = 1e-5
SCALED = (0, 2, 2)
SLOPE = 1.702

FLOPS = 2 * HEADS * EXPERTS * DIM * DIM * TOKENS
BYTES = (
    EXPERTS * TOKENS * HEADS * DIM * 2
    + TOKENS * HEADS * EXPERTS * DIM * (4 + 2)
    + 2 * HEADS * EXPERTS * DIM * 2
    + HEADS * EXPERTS * DIM * DIM * 4
)


def by_token(rows):
    return rows.rearrange("(p j) w -> p j w", j=PACK)


def token_major(tile_ap):
    return tile_ap.rearrange("p j (r i) -> p r j i", i=RUN)


def column_major(tile_ap):
    return tile_ap.rearrange("p (r i) j -> p r j i", i=RUN)


def tile_mom_v_kernel(
    tc, x1, x2, x3, W, b, gamma, beta, running_mean, running_var, y, grad_out, out
):
    nc = tc.nc
    xs = (x1, x2, x3)

    groups = [(e, c) for e in range(EXPERTS) for c in range(PASSES)]
    chunks = [(e, c, h) for e in range(EXPERTS - 1) for c in range(PASSES) for h in range(HEADS)]
    chunks += [(EXPERTS - 1, c, h) for h in range(HEADS) for c in range(PASSES)]
    n_chunks = len(chunks)
    last = n_chunks - 1
    whole = [slice(0, DIM)]
    tiles_of_128 = [slice(m * P, (m + 1) * P) for m in range(F_TILES)]
    turned = slice(0, TURNED * P)
    straight = slice(TURNED * P, DIM)

    with ExitStack() as ctx:
        const = ctx.enter_context(tc.tile_pool(name="const", bufs=1))
        y_pool = ctx.enter_context(tc.tile_pool(name="y", bufs=3))
        g_pool = ctx.enter_context(tc.tile_pool(name="g", bufs=3))
        x_in_pool = ctx.enter_context(tc.tile_pool(name="x_in", bufs=3))
        work = ctx.enter_context(tc.tile_pool(name="work", bufs=3))
        x_pool = ctx.enter_context(tc.tile_pool(name="x_grouped", bufs=2))
        dy_pool = ctx.enter_context(tc.tile_pool(name="dy_grouped", bufs=3))
        quantised = ctx.enter_context(tc.tile_pool(name="quantised", bufs=2))
        result_pool = ctx.enter_context(tc.tile_pool(name="result", bufs=2 * F_TILES))
        psum_y = ctx.enter_context(tc.psum_pool(name="psum_y", bufs=2))
        psum_a = ctx.enter_context(tc.psum_pool(name="psum_a", bufs=2))
        psum_coef = ctx.enter_context(tc.psum_pool(name="psum_coef", bufs=2))
        psum_out = ctx.enter_context(tc.psum_pool(name="psum_out", bufs=2))
        ctx.enter_context(tc.manual_schedule())

        n_rows = HEADS * EXPERTS * F_TILES
        var_rows = const.tile([n_rows, P], BF16)
        row_blocks = [slice(0, 16), slice(16, n_rows)]
        for rows in row_blocks:
            nc.sync.dma_start(
                out=var_rows[rows, :], in_=running_var.rearrange("h e (m p) -> (h e m) p", p=P)[rows, :]
            )
        gamma_rows = const.tile([n_rows, P], BF16)
        for rows in row_blocks:
            nc.sync.dma_start(
                out=gamma_rows[rows, :], in_=gamma.rearrange("h e (m p) -> (h e m) p", p=P)[rows, :]
            )
        coef_rows = const.tile([P, P], F32)
        nc.vector.memset(coef_rows[:], 0.0)
        ident_f32 = const.tile([P, P], F32)
        make_identity(nc, ident_f32[:])

        def group_of(i):
            e, c, h = chunks[i]
            return PASSES * e + c

        first_use = {}
        for i in range(n_chunks):
            if chunks[i][2] == 0:
                first_use[i] = group_of(i)

        y_tiles = {}
        g_tiles = {}
        x_tiles = {}

        def new_y(k):
            y_tile = y_pool.tile([P, PACK, HEADS * DIM], F32)
            y_tiles[k] = y_tile

        def load_y(k, cols):
            e, c = groups[k]
            tokens = slice(c * K_PASS, (c + 1) * K_PASS)
            col0 = e * HEADS * DIM
            nc.sync.dma_start(
                out=y_tiles[k][:, :, cols], in_=by_token(y[tokens, col0 + cols.start : col0 + cols.stop])
            )

        def y_columns(i, cols):
            h = chunks[i][2]
            return y_tiles[group_of(i)][:, :, h * DIM + cols.start : h * DIM + cols.stop]

        def new_g(k):
            g_tile = g_pool.tile([P, PACK, HEADS * DIM], BF16)
            g_tiles[k] = g_tile

        def new_x(k):
            x_tile = x_in_pool.tile([P, PACK, HEADS * DIM], BF16)
            x_tiles[k] = x_tile

        def load_g(k, cols):
            e, c = groups[k]
            tokens = slice(c * K_PASS, (c + 1) * K_PASS)
            col0 = e * HEADS * DIM
            nc.sync.dma_start(
                out=g_tiles[k][:, :, cols], in_=by_token(grad_out[tokens, col0 + cols.start : col0 + cols.stop])
            )

        def load_x(k, cols):
            e, c = groups[k]
            tokens = slice(c * K_PASS, (c + 1) * K_PASS)
            nc.sync.dma_start(out=x_tiles[k][:, :, cols], in_=by_token(xs[e][tokens, cols]))

        both_heads = slice(0, HEADS * DIM)

        head_cols = [slice(h * DIM, (h + 1) * DIM) for h in range(HEADS)]
        for k in range(PASSES):
            new_y(k)
            new_x(k)
            new_g(k)
        load_y(0, straight)
        load_y(0, turned)
        load_x(0, head_cols[0])
        load_y(0, head_cols[1])
        load_x(0, head_cols[1])
        load_g(0, head_cols[0])
        load_y(1, head_cols[0])
        load_x(1, head_cols[0])
        load_g(0, head_cols[1])
        load_y(1, head_cols[1])
        load_x(1, head_cols[1])

        first_sqrt = const.tile([P, 1], F32)
        nc.scalar.activation(out=first_sqrt[:], in_=coef_rows[:, 0:1], func=ACT.Sqrt)
        std = const.tile([n_rows, P], F32)
        nc.scalar.activation(out=std[:], in_=var_rows[:], func=ACT.Sqrt, bias=EPS)
        inv_std = const.tile([n_rows, P], F32)
        nc.vector.reciprocal(out=inv_std[:], in_=std[:])
        nc.vector.scalar_tensor_tensor(
            out=coef_rows[0:n_rows, :], in0=gamma_rows[:], scalar=-0.5, in1=inv_std[:], op0=ALU.mult, op1=ALU.mult
        )
        coef_bank = psum_a.tile([P, DIM], F32, name="by_tokens")
        nc.tensor.transpose(coef_bank[:, 0:P], coef_rows[:], ident_f32[:])
        coef = const.tile([P, n_rows], F32)
        nc.vector.tensor_copy(out=coef[:], in_=coef_bank[:, 0:n_rows])

        codes = {}
        coef_all = {}

        def spread_coef(e, h, m):
            if (h, m) == (0, TURNED):
                coef_all[e] = psum_coef.tile([P, HEADS, F_TILES - TURNED, P], F32, name="coef_all")
            row = (EXPERTS * h + e) * F_TILES + m
            nc.tensor.matmul(
                out=coef_all[e][:, h, m - TURNED, :],
                lhsT=ident_f32[:, row : row + 1].to_broadcast([P, P]),
                rhs=coef_rows[:],
                start=True,
                stop=True,
            )

        def start_expert(e):
            dy_codes = quantised.tile([P, HEADS, PASSES, DIM], U32, align_bytes=64)
            dy_scales = quantised.tile([P, HEADS, PASSES, DIM], U8, align_bytes=64)
            x_codes = quantised.tile([P, HEADS, PASSES, DIM], U32, align_bytes=64)
            x_scales = quantised.tile([P, HEADS, PASSES, DIM], U8, align_bytes=64)
            codes[e] = (dy_codes, dy_scales, x_codes, x_scales)

        tanh_turned = {}
        tanh_straight = {}
        silu_part = {}
        x_grouped = {}
        dy_grouped = {}
        by_features = {}
        by_tokens = {}

        def turn_y(i, m):
            bank = psum_y.tile([P, PACK, P], F32, name="by_features")
            for j in range(PACK):
                nc.tensor.transpose(bank[:, j, :], y_columns(i, tiles_of_128[m])[:, j, :], ident_f32[:])
            by_features[(i, m)] = bank

        def start_chunk(i):
            e, c, h = chunks[i]
            tanh_turned[i] = work.tile([P, TURNED, PACK * P], F32, name="tanh_turned")
            tanh_straight[i] = work.tile([P, PACK, DIM - TURNED * P], F32, name="tanh_straight")
            silu_part[i] = work.tile([P, PACK, DIM], F32, name="silu_part")

        def take_tanh_turned(i, m):
            nc.scalar.activation(
                out=tanh_turned[i][:, m, :],
                in_=by_features[(i, m)][:].rearrange("f j p -> f (j p)"),
                func=ACT.Tanh,
                scale=SLOPE / 2,
            )

        def take_tanh_straight(i):
            nc.scalar.activation(
                out=tanh_straight[i][:], in_=y_columns(i, straight), func=ACT.Tanh, scale=SLOPE / 2
            )

        def take_silu(i, cols):
            nc.scalar.activation(
                out=silu_part[i][:, :, cols], in_=y_columns(i, cols), func=ACT.Silu, scale=-SLOPE
            )

        def coef_column(i, m):
            e, c, h = chunks[i]
            row = (EXPERTS * h + e) * F_TILES + m
            return coef[:, row : row + 1]

        def times_coef_vector(i, m):
            nc.vector.tensor_scalar(
                out=tanh_turned[i][:, m, :],
                in0=tanh_turned[i][:, m, :],
                scalar1=1.0,
                scalar2=coef_column(i, m),
                op0=ALU.add,
                op1=ALU.mult,
            )

        def times_coef_scalar(i, m):
            nc.scalar.activation(
                out=tanh_turned[i][:, m, :],
                in_=tanh_turned[i][:, m, :],
                func=ACT.Identity,
                scale=coef_column(i, m),
                bias=coef_column(i, m),
            )

        def turn_back(i, m):
            bank = psum_a.tile([P, PACK, P], F32, name="by_tokens")
            for j in range(PACK):
                nc.tensor.transpose(bank[:, j, :], tanh_turned[i][:, m, j * P : (j + 1) * P], ident_f32[:])
            by_tokens[(i, m)] = bank

        def first_multiply_straight(i):
            e, c, h = chunks[i]
            row_coef = coef_all[e][:, h, :, :].rearrange("p m f -> p (m f)")
            nc.vector.scalar_tensor_tensor(
                out=tanh_straight[i][:],
                in0=tanh_straight[i][:],
                scalar=1.0,
                in1=row_coef.unsqueeze(1).to_broadcast([P, PACK, DIM - TURNED * P]),
                op0=ALU.add,
                op1=ALU.mult,
            )

        def second_multiply(i, cols, factor):
            nc.vector.scalar_tensor_tensor(
                out=silu_part[i][:, :, cols],
                in0=silu_part[i][:, :, cols],
                scalar=1.0,
                in1=factor[:],
                op0=ALU.subtract,
                op1=ALU.mult,
            )

        def second_multiply_turned(i, m):
            second_multiply(i, tiles_of_128[m], by_tokens[(i, m)])

        def second_multiply_straight(i):
            second_multiply(i, straight, tanh_straight[i])

        def third_multiply(i, cols):
            e, c, h = chunks[i]
            if i not in dy_grouped:
                dy_grouped[i] = dy_pool.tile([P, DIM, PACK], BF16, name="dy_grouped", align_bytes=64)
            nc.vector.tensor_tensor(
                out=column_major(dy_grouped[i][:, cols, :]),
                in0=token_major(silu_part[i][:, :, cols]),
                in1=token_major(g_tiles[group_of(i)][:, :, h * DIM + cols.start : h * DIM + cols.stop]),
                op=ALU.mult,
            )

        def regroup_x(i, cols, copy):
            e, c, h = chunks[i]
            copy(
                out=column_major(x_grouped[i][:, cols, :]),
                in_=token_major(x_tiles[group_of(i)][:, :, h * DIM + cols.start : h * DIM + cols.stop]),
            )

        def new_x_grouped(i):
            x_grouped[i] = x_pool.tile([P, DIM, PACK], BF16, name="x_grouped", align_bytes=64)

        def regroup_x_gpsimd(i, cols):
            e, c, h = chunks[i]
            nc.gpsimd.tensor_scalar(
                out=x_grouped[i][:, cols, :],
                in0=x_tiles[group_of(i)][:, :, h * DIM + cols.start : h * DIM + cols.stop].rearrange("p j w -> p w j"),
                scalar1=1.0,
                scalar2=0.0,
                op0=ALU.mult,
                op1=ALU.add,
            )

        def quantise_x(i):
            e, c, h = chunks[i]
            x_codes, x_scales = codes[e][2:4]
            nc.vector.quantize_mx(
                out=x_codes[:, h, c, :].bitcast(E4M3_X4),
                scales=x_scales[:, h, c, :],
                in_=x_grouped[i][:].rearrange("p w j -> p (w j)"),
            )

        def quantise_dy(i, cols):
            e, c, h = chunks[i]
            dy_codes, dy_scales = codes[e][0:2]
            nc.vector.quantize_mx(
                out=dy_codes[:, h, c, cols].bitcast(E5M2_X4),
                scales=dy_scales[:, h, c, cols],
                in_=dy_grouped[i][:, cols, :].rearrange("p w j -> p (w j)"),
            )

        accs = {}

        def multiply(i, m):
            e, c, h = chunks[i]
            dy_codes, dy_scales, x_codes, x_scales = codes[e]
            f_cols = tiles_of_128[m]
            acc = psum_out.tile([P, DIM], F32)
            for k in range(PASSES):
                nc.tensor.matmul_mx(
                    out=acc[:],
                    lhsT=dy_codes[:, h, k, f_cols].bitcast(E5M2_X4),
                    lhsT_scale=dy_scales[:, h, k, f_cols],
                    rhs=x_codes[:, h, k, :].bitcast(E4M3_X4),
                    rhs_scale=x_scales[:, h, k, :],
                    start=(k == 0),
                    stop=(k == PASSES - 1),
                )
            accs[(i, m)] = acc

        def store(i, m):
            e, c, h = chunks[i]
            result = result_pool.tile([P, DIM], F32)
            nc.scalar.copy(out=result[:], in_=accs[(i, m)][:])
            nc.sync.dma_start(out=out[h, e, tiles_of_128[m], :], in_=result[:])

        def pair_done(i):
            return i >= 0 and chunks[i][1] == PASSES - 1

        g_share = slice(0, G_COLS)
        s_share = slice(G_COLS, DIM)

        spread_order = [(e, h, m) for e in range(EXPERTS) for h in range(HEADS) for m in range(TURNED, F_TILES)]
        per_expert = HEADS * (F_TILES - TURNED)
        for k in range(per_expert):
            spread_coef(*spread_order[k])
        start_expert(0)
        new_x_grouped(0)
        start_chunk(0)
        take_tanh_straight(0)
        first_multiply_straight(0)
        take_silu(0, straight)
        for m in range(TURNED):
            turn_y(0, m)
        second_multiply_straight(0)
        for m in range(TURNED):
            take_tanh_turned(0, m)
        for m in range(TURNED):
            times_coef_vector(0, m)
            turn_back(0, m)
        for m in range(TURNED):
            turn_y(1, m)
        spread_coef(*spread_order[per_expert])
        take_silu(0, turned)
        regroup_x(0, whole[0], nc.vector.tensor_copy)
        new_y(2)
        load_y(2, head_cols[0])
        load_g(1, both_heads)
        load_y(2, head_cols[1])
        start_chunk(1)
        take_tanh_straight(1)
        for m in range(TURNED):
            take_tanh_turned(1, m)
            turn_y(2, m)
        for m in range(TURNED - SCALED[0], TURNED):
            times_coef_scalar(1, m)
        take_silu(1, whole[0])
        in_flight = []
        waiting = []
        for i in range(n_chunks):
            if i > 0:
                quantise_x(i - 1)
            if i + 1 < n_chunks:
                new_x_grouped(i + 1)
                regroup_x_gpsimd(i + 1, g_share)
            for m in range(TURNED):
                second_multiply_turned(i, m)
            if i + 1 < n_chunks:
                first_multiply_straight(i + 1)
            if i + 2 < n_chunks:
                start_chunk(i + 2)
                if chunks[i + 2][1:] == (0, 0):
                    start_expert(chunks[i + 2][0])
                for m in range(TURNED):
                    take_tanh_turned(i + 2, m)
                take_tanh_straight(i + 2)
                for m in range(TURNED - SCALED[chunks[i + 2][0]], TURNED):
                    times_coef_scalar(i + 2, m)
                take_silu(i + 2, whole[0])
            if i + 4 in first_use:
                new_x(first_use[i + 4])
                load_x(first_use[i + 4], both_heads)
            if i + 6 in first_use:
                new_y(first_use[i + 6])
                load_y(first_use[i + 6], both_heads)
            if i + 1 < n_chunks:
                for m in range(TURNED - SCALED[chunks[i + 1][0]]):
                    times_coef_vector(i + 1, m)
                for m in range(TURNED):
                    turn_back(i + 1, m)
            if i + 3 < n_chunks:
                for m in range(TURNED):
                    turn_y(i + 3, m)
            if i > 0:
                second_multiply_straight(i)
            if i >= 1:
                quantise_dy(i - 1, whole[0])
            if pair_done(i - 1):
                waiting += [(i - 1, m) for m in range(F_TILES)]
            for turn in range(1 + (len(waiting) > F_TILES)):
                for tile in in_flight:
                    store(*tile)
                in_flight = waiting[:2]
                waiting = waiting[2:]
                for tile in in_flight:
                    multiply(*tile)
            if i < last:
                third_multiply(i, whole[0])
            else:
                quantise_x(i)
            if per_expert + 1 + i < len(spread_order):
                spread_coef(*spread_order[per_expert + 1 + i])
            if i + 1 < n_chunks:
                regroup_x(i + 1, s_share, nc.scalar.copy)
            if i + 3 in first_use and first_use[i + 3] >= PASSES:
                new_g(first_use[i + 3])
                load_g(first_use[i + 3], both_heads)
        for tile in in_flight:
            store(*tile)
        for m in range(F_TILES):
            third_multiply(last, tiles_of_128[m])
            quantise_dy(last, tiles_of_128[m])
            multiply(last, m)
            store(last, m)
